import numpy as np
import ml_dtypes

BF16 = ml_dtypes.bfloat16


def bf(x):
    return np.asarray(x, np.float32).astype(BF16)


def f32(x):
    return np.asarray(x, np.float32)


def f64(x):
    return np.asarray(x).astype(np.float64)


def striped(idx):
    return np.tile(idx.reshape(-1, 16).T, (8, 1))


D, S, M, K, P, N = 128, 512, 256, 128, 2, 256
SIGMA = 0.25


def setup_inputs():
    return {"table": bf(np.random.standard_normal((D, S))), "w": bf(SIGMA * np.random.standard_normal((D, M)) / np.sqrt(D)), "b": f32(0.5 * np.pi * np.random.uniform(size=(M, 1))), "offs": striped(np.random.permutation(S)[:N])}


def reference(table, w, b, offs):
    idx = offs[:16].T.reshape(-1)
    theta = f64(w).T @ f64(table)[:, idx] + f64(b)
    c = np.cos(0.5 * theta) ** 2
    s = np.sin(0.5 * theta) ** 2
    o = 0.5 * np.sin(theta)
    rot = np.stack([c, o, -o, s]).reshape(P, P, K, P, N)
    planes = []
    for a in range(P):
        for cc in range(P):
            for bb in range(P):
                for d in range(P):
                    sign = -1.0 if (a != bb and cc != d) else 1.0
                    planes.append(sign * rot[a, bb, :, 0, :] * rot[cc, d, :, 1, :])
    return np.concatenate(planes, axis=0)

@@ -1,0 +1,59 @@
+import math
+
+import concourse.mybir as mybir
+
+F32, BF16, U16 = mybir.dt.float32, mybir.dt.bfloat16, mybir.dt.uint16
+SIN = mybir.ActivationFunctionType.Sin
+MULT, ADD = mybir.AluOpType.mult, mybir.AluOpType.add
+
+D, S, M, N = 128, 512, 256, 256
+K = M // 2
+FLOPS = 2 * D * M * N
+
+
+def tile_featureencodinglayer_kernel(tc, table, w, b, offs, out):
+    nc = tc.nc
+    with tc.tile_pool(name="held", bufs=1) as held, tc.psum_pool(name="psum", bufs=1) as psum:
+        offsets = held.tile([128, N // 16], U16, name="offsets")
+        nc.sync.dma_start(offsets[:], offs)
+        table_sb = held.tile([D, S], BF16, name="table_sb")
+        nc.sync.dma_start(table_sb[:], table)
+        w_sb = held.tile([D, K, 2], BF16, name="w_sb")
+        nc.scalar.dma_start(w_sb[:], w.rearrange("d (k u) -> d k u", u=2))
+        w_units = held.tile([D, 2, K], BF16, name="w_units")
+        nc.vector.tensor_copy(w_units[:], w_sb[:].rearrange("d k u -> d u k"))
+        b_sb = held.tile([K, 2], F32, name="b_sb")
+        nc.scalar.dma_start(b_sb[:], b.rearrange("(k u) o -> k (u o)", u=2))
+
+        sin_bias = held.tile([K, 2], F32, name="sin_bias")
+        nc.vector.tensor_scalar(sin_bias[:], b_sb[:], 0.5, None, MULT)
+        cos_bias = held.tile([K, 2], F32, name="cos_bias")
+        nc.vector.tensor_scalar(cos_bias[:], b_sb[:], 0.5, math.pi / 2, MULT, ADD)
+
+        half_sin = held.tile([K, 2, N], F32, name="half_sin")
+        half_cos = held.tile([K, 2, N], F32, name="half_cos")
+        for u in range(2):
+            angle = psum.tile([K, N], F32, name=f"angle{u}")
+            nc.tensor.matmul(angle[:], w_units[:, u, :], table_sb[:].indirect(offsets[:]), start=True, stop=True)
+            nc.scalar.activation(half_cos[:, u, :], angle[:], SIN, bias=cos_bias[:, u : u + 1], scale=0.5)
+            nc.scalar.activation(half_sin[:, u, :], angle[:], SIN, bias=sin_bias[:, u : u + 1], scale=0.5)
+
+        c = held.tile([K, 2, N], F32, name="c")
+        nc.vector.tensor_tensor(c[:], half_cos[:], half_cos[:], MULT)
+        o = held.tile([K, 2, N], F32, name="o")
+        nc.vector.tensor_tensor(o[:], half_sin[:], half_cos[:], MULT)
+        minus_o = held.tile([K, 2, N], F32, name="minus_o")
+        nc.vector.tensor_scalar(minus_o[:], o[:], -1.0, None, MULT)
+        s = held.tile([K, 2, N], F32, name="s")
+        nc.vector.tensor_tensor(s[:], half_sin[:], half_sin[:], MULT)
+        rotation = ((c, o), (minus_o, s))
+        flipped = ((c, minus_o), (o, s))
+
+        out_rows = out.rearrange("(r q k) j -> r k q j", q=4, k=K)
+        for r in range(4):
+            row = held.tile([K, 4, N], F32, name=f"row{r}")
+            for q in range(4):
+                a, cc, bb, d = r // 2, r % 2, q // 2, q % 2
+                factor_b = flipped if a != bb else rotation
+                nc.vector.tensor_tensor(row[:, q, :], rotation[a][bb][:, 0, :], factor_b[cc][d][:, 1, :], MULT)
+            nc.sync.dma_start(out_rows[r], row[:])

@@ -3,7 +3,7 @@ import math
 import concourse.mybir as mybir
 
 F32, BF16, U16 = mybir.dt.float32, mybir.dt.bfloat16, mybir.dt.uint16
-SIN = mybir.ActivationFunctionType.Sin
+SIN, SQUARE = mybir.ActivationFunctionType.Sin, mybir.ActivationFunctionType.Square
 MULT, ADD = mybir.AluOpType.mult, mybir.AluOpType.add
 
 D, S, M, N = 128, 512, 256, 256
@@ -25,35 +25,55 @@ def tile_featureencodinglayer_kernel(tc, table, w, b, offs, out):
         b_sb = held.tile([K, 2], F32, name="b_sb")
         nc.scalar.dma_start(b_sb[:], b.rearrange("(k u) o -> k (u o)", u=2))
 
+        scratch = held.tile([K, 1], F32, name="scratch")
+        nc.vector.memset(scratch[:], 0.0)
+        nc.scalar.activation(scratch[:], scratch[:], SIN)
+
         sin_bias = held.tile([K, 2], F32, name="sin_bias")
         nc.vector.tensor_scalar(sin_bias[:], b_sb[:], 0.5, None, MULT)
         cos_bias = held.tile([K, 2], F32, name="cos_bias")
         nc.vector.tensor_scalar(cos_bias[:], b_sb[:], 0.5, math.pi / 2, MULT, ADD)
 
-        half_sin = held.tile([K, 2, N], F32, name="half_sin")
-        half_cos = held.tile([K, 2, N], F32, name="half_cos")
-        for u in range(2):
-            angle = psum.tile([K, N], F32, name=f"angle{u}")
-            nc.tensor.matmul(angle[:], w_units[:, u, :], table_sb[:].indirect(offsets[:]), start=True, stop=True)
-            nc.scalar.activation(half_cos[:, u, :], angle[:], SIN, bias=cos_bias[:, u : u + 1], scale=0.5)
-            nc.scalar.activation(half_sin[:, u, :], angle[:], SIN, bias=sin_bias[:, u : u + 1], scale=0.5)
+        angle_a = psum.tile([K, N], F32, name="angle_a")
+        angle_b = psum.tile([K, N], F32, name="angle_b")
+        nc.tensor.matmul(angle_a[:], w_units[:, 0, :], table_sb[:].indirect(offsets[:]), start=True, stop=True)
+        nc.tensor.matmul(angle_b[:], w_units[:, 1, :], table_sb[:].indirect(offsets[:]), start=True, stop=True)
 
-        c = held.tile([K, 2, N], F32, name="c")
-        nc.vector.tensor_tensor(c[:], half_cos[:], half_cos[:], MULT)
-        o = held.tile([K, 2, N], F32, name="o")
-        nc.vector.tensor_tensor(o[:], half_sin[:], half_cos[:], MULT)
-        minus_o = held.tile([K, 2, N], F32, name="minus_o")
-        nc.vector.tensor_scalar(minus_o[:], o[:], -1.0, None, MULT)
-        s = held.tile([K, 2, N], F32, name="s")
-        nc.vector.tensor_tensor(s[:], half_sin[:], half_sin[:], MULT)
-        rotation = ((c, o), (minus_o, s))
-        flipped = ((c, minus_o), (o, s))
+        trig_a = held.tile([K, 2, N], F32, name="trig_a")
+        trig_b = held.tile([K, 2, N], F32, name="trig_b")
+        nc.scalar.activation(trig_a[:, 0, :], angle_a[:], SIN, bias=cos_bias[:, 0:1], scale=0.5)
+        nc.scalar.activation(trig_b[:, 0, :], angle_b[:], SIN, bias=cos_bias[:, 1:2], scale=0.5)
+        nc.scalar.activation(trig_b[:, 1, :], angle_b[:], SIN, bias=sin_bias[:, 1:2], scale=0.5)
+        nc.scalar.activation(trig_a[:, 1, :], angle_a[:], SIN, bias=sin_bias[:, 0:1], scale=0.5)
 
-        out_rows = out.rearrange("(r q k) j -> r k q j", q=4, k=K)
-        for r in range(4):
-            row = held.tile([K, 4, N], F32, name=f"row{r}")
-            for q in range(4):
-                a, cc, bb, d = r // 2, r % 2, q // 2, q % 2
-                factor_b = flipped if a != bb else rotation
-                nc.vector.tensor_tensor(row[:, q, :], rotation[a][bb][:, 0, :], factor_b[cc][d][:, 1, :], MULT)
-            nc.sync.dma_start(out_rows[r], row[:])
+        v = held.tile([K, 4, N], F32, name="v")
+        nc.vector.tensor_tensor(v[:, 0:2, :], trig_a[:, 0:1, :].to_broadcast([K, 2, N]), trig_b[:], MULT)
+        nc.vector.tensor_tensor(v[:, 2, :], trig_a[:, 1, :], trig_b[:, 0, :], MULT)
+        nc.vector.scalar_tensor_tensor(v[:, 3, :], trig_a[:, 1, :], -1.0, trig_b[:, 1, :], MULT, MULT)
+
+        planes = out.rearrange("(e k) j -> k e j", k=K)
+
+        diagonal = held.tile([K, 4, N], F32, name="diagonal")
+        nc.scalar.activation(diagonal[:, 0:2, :], v[:, 0:2, :], SQUARE)
+        nc.sync.dma_start(planes[:, 0:6:5, :], diagonal[:, 0:2, :])
+        nc.scalar.activation(diagonal[:, 2:4, :], v[:, 2:4, :], SQUARE)
+        nc.sync.dma_start(planes[:, 10:16:5, :], diagonal[:, 2:4, :])
+
+        row0 = held.tile([K, 3, N], F32, name="row0")
+        nc.vector.tensor_tensor(row0[:], v[:, 0:1, :].to_broadcast([K, 3, N]), v[:, 1:4, :], MULT)
+        nc.sync.dma_start(planes[:, 1:4, :], row0[:])
+        column0 = held.tile([K, 2, N], F32, name="column0")
+        nc.scalar.mul(column0[:], row0[:, 0:2, :], -1.0)
+        nc.sync.dma_start(planes[:, 4:9:4, :], column0[:])
+
+        row3 = held.tile([K, 3, N], F32, name="row3")
+        nc.vector.tensor_tensor(row3[:], v[:, 3:4, :].to_broadcast([K, 3, N]), v[:, 0:3, :], MULT)
+        nc.sync.dma_start(planes[:, 12:15, :], row3[:])
+        column3 = held.tile([K, 2, N], F32, name="column3")
+        nc.scalar.mul(column3[:], row3[:, 1:3, :], -1.0)
+        nc.sync.dma_start(planes[:, 7:12:4, :], column3[:])
+
+        centre = held.tile([K, N], F32, name="centre")
+        nc.vector.tensor_tensor(centre[:], v[:, 1, :], v[:, 2, :], MULT)
+        nc.sync.dma_start(planes[:, 6, :], centre[:])
+        nc.sync.dma_start(planes[:, 9, :], centre[:])

@@ -9,6 +9,7 @@ MULT, ADD = mybir.AluOpType.mult, mybir.AluOpType.add
 D, S, M, N = 128, 512, 256, 256
 K = M // 2
 FLOPS = 2 * D * M * N
+NEGATED = ((1, 0), (2, 0), (1, 3), (2, 3))
 
 
 def tile_featureencodinglayer_kernel(tc, table, w, b, offs, out):
@@ -39,41 +40,45 @@ def tile_featureencodinglayer_kernel(tc, table, w, b, offs, out):
         nc.tensor.matmul(angle_a[:], w_units[:, 0, :], table_sb[:].indirect(offsets[:]), start=True, stop=True)
         nc.tensor.matmul(angle_b[:], w_units[:, 1, :], table_sb[:].indirect(offsets[:]), start=True, stop=True)
 
-        trig_a = held.tile([K, 2, N], F32, name="trig_a")
-        trig_b = held.tile([K, 2, N], F32, name="trig_b")
-        nc.scalar.activation(trig_a[:, 0, :], angle_a[:], SIN, bias=cos_bias[:, 0:1], scale=0.5)
-        nc.scalar.activation(trig_b[:, 0, :], angle_b[:], SIN, bias=cos_bias[:, 1:2], scale=0.5)
-        nc.scalar.activation(trig_b[:, 1, :], angle_b[:], SIN, bias=sin_bias[:, 1:2], scale=0.5)
-        nc.scalar.activation(trig_a[:, 1, :], angle_a[:], SIN, bias=sin_bias[:, 0:1], scale=0.5)
+        trig = {name: held.tile([K, N], F32, name=name) for name in ("cos_a", "cos_b", "sin_a", "sin_b")}
+        sources = {
+            "cos_a": (angle_a, cos_bias[:, 0:1]),
+            "sin_a": (angle_a, sin_bias[:, 0:1]),
+            "cos_b": (angle_b, cos_bias[:, 1:2]),
+            "sin_b": (angle_b, sin_bias[:, 1:2]),
+        }
 
-        v = held.tile([K, 4, N], F32, name="v")
-        nc.vector.tensor_tensor(v[:, 0:2, :], trig_a[:, 0:1, :].to_broadcast([K, 2, N]), trig_b[:], MULT)
-        nc.vector.tensor_tensor(v[:, 2, :], trig_a[:, 1, :], trig_b[:, 0, :], MULT)
-        nc.vector.scalar_tensor_tensor(v[:, 3, :], trig_a[:, 1, :], -1.0, trig_b[:, 1, :], MULT, MULT)
+        def half_angle_sine(name):
+            angle, bias = sources[name]
+            nc.scalar.activation(trig[name][:], angle[:], SIN, bias=bias, scale=0.5)
 
-        planes = out.rearrange("(e k) j -> k e j", k=K)
+        planes = out.rearrange("(e k) j -> e k j", k=K)
 
-        diagonal = held.tile([K, 4, N], F32, name="diagonal")
-        nc.scalar.activation(diagonal[:, 0:2, :], v[:, 0:2, :], SQUARE)
-        nc.sync.dma_start(planes[:, 0:6:5, :], diagonal[:, 0:2, :])
-        nc.scalar.activation(diagonal[:, 2:4, :], v[:, 2:4, :], SQUARE)
-        nc.sync.dma_start(planes[:, 10:16:5, :], diagonal[:, 2:4, :])
-
-        row0 = held.tile([K, 3, N], F32, name="row0")
-        nc.vector.tensor_tensor(row0[:], v[:, 0:1, :].to_broadcast([K, 3, N]), v[:, 1:4, :], MULT)
-        nc.sync.dma_start(planes[:, 1:4, :], row0[:])
-        column0 = held.tile([K, 2, N], F32, name="column0")
-        nc.scalar.mul(column0[:], row0[:, 0:2, :], -1.0)
-        nc.sync.dma_start(planes[:, 4:9:4, :], column0[:])
-
-        row3 = held.tile([K, 3, N], F32, name="row3")
-        nc.vector.tensor_tensor(row3[:], v[:, 3:4, :].to_broadcast([K, 3, N]), v[:, 0:3, :], MULT)
-        nc.sync.dma_start(planes[:, 12:15, :], row3[:])
-        column3 = held.tile([K, 2, N], F32, name="column3")
-        nc.scalar.mul(column3[:], row3[:, 1:3, :], -1.0)
-        nc.sync.dma_start(planes[:, 7:12:4, :], column3[:])
-
-        centre = held.tile([K, N], F32, name="centre")
-        nc.vector.tensor_tensor(centre[:], v[:, 1, :], v[:, 2, :], MULT)
-        nc.sync.dma_start(planes[:, 6, :], centre[:])
-        nc.sync.dma_start(planes[:, 9, :], centre[:])
+        factors = (("cos_a", "cos_b"), ("cos_a", "sin_b"), ("sin_a", "cos_b"), ("sin_a", "sin_b"))
+        new_sines = (("cos_a", "cos_b"), ("sin_b",), ("sin_a",), ())
+        for name in new_sines[0]:
+            half_angle_sine(name)
+        v = []
+        for q in range(4):
+            for name in new_sines[q + 1] if q < 3 else ():
+                half_angle_sine(name)
+            of_a, of_b = factors[q]
+            term = held.tile([K, N], F32, name=f"v{q}")
+            if q < 3:
+                nc.vector.tensor_tensor(term[:], trig[of_a][:], trig[of_b][:], MULT)
+            else:
+                nc.vector.scalar_tensor_tensor(term[:], trig[of_a][:], -1.0, trig[of_b][:], MULT, MULT)
+            v.append(term)
+            square = held.tile([K, N], F32, name=f"square{q}")
+            nc.scalar.activation(square[:], term[:], SQUARE)
+            nc.sync.dma_start(planes[5 * q], square[:])
+            for r in range(q):
+                product = held.tile([K, N], F32, name=f"product{r}{q}")
+                nc.vector.tensor_tensor(product[:], v[r][:], term[:], MULT)
+                for row, col in ((r, q), (q, r)):
+                    if (row, col) in NEGATED:
+                        minus = held.tile([K, N], F32, name=f"minus{r}{q}")
+                        nc.scalar.mul(minus[:], product[:], -1.0)
+                        nc.sync.dma_start(planes[4 * row + col], minus[:])
+                    else:
+                        nc.sync.dma_start(planes[4 * row + col], product[:])

@@ -10,6 +10,7 @@ D, S, M, N = 128, 512, 256, 256
 K = M // 2
 FLOPS = 2 * D * M * N
 NEGATED = ((1, 0), (2, 0), (1, 3), (2, 3))
+H = 128
 
 
 def tile_featureencodinglayer_kernel(tc, table, w, b, offs, out):
@@ -21,8 +22,10 @@ def tile_featureencodinglayer_kernel(tc, table, w, b, offs, out):
         nc.sync.dma_start(table_sb[:], table)
         w_sb = held.tile([D, K, 2], BF16, name="w_sb")
         nc.scalar.dma_start(w_sb[:], w.rearrange("d (k u) -> d k u", u=2))
-        w_units = held.tile([D, 2, K], BF16, name="w_units")
-        nc.vector.tensor_copy(w_units[:], w_sb[:].rearrange("d k u -> d u k"))
+        w_a = held.tile([D, K], BF16, name="w_a")
+        nc.vector.tensor_copy(w_a[:], w_sb[:, :, 0])
+        w_b = held.tile([D, K], BF16, name="w_b")
+        nc.vector.tensor_copy(w_b[:], w_sb[:, :, 1])
         b_sb = held.tile([K, 2], F32, name="b_sb")
         nc.scalar.dma_start(b_sb[:], b.rearrange("(k u) o -> k (u o)", u=2))
 
@@ -35,50 +38,52 @@ def tile_featureencodinglayer_kernel(tc, table, w, b, offs, out):
         cos_bias = held.tile([K, 2], F32, name="cos_bias")
         nc.vector.tensor_scalar(cos_bias[:], b_sb[:], 0.5, math.pi / 2, MULT, ADD)
 
-        angle_a = psum.tile([K, N], F32, name="angle_a")
-        angle_b = psum.tile([K, N], F32, name="angle_b")
-        nc.tensor.matmul(angle_a[:], w_units[:, 0, :], table_sb[:].indirect(offsets[:]), start=True, stop=True)
-        nc.tensor.matmul(angle_b[:], w_units[:, 1, :], table_sb[:].indirect(offsets[:]), start=True, stop=True)
+        pieces = [slice(h * H, (h + 1) * H) for h in range(N // H)]
+        angle_a, angle_b = [], []
+        for h in range(N // H):
+            looked_up = table_sb[:].indirect(offsets[:, h * (H // 16) : (h + 1) * (H // 16)])
+            angle_a.append(psum.tile([K, H], F32, name=f"angle_a{h}"))
+            nc.tensor.matmul(angle_a[h][:], w_a[:], looked_up, start=True, stop=True)
+            angle_b.append(psum.tile([K, H], F32, name=f"angle_b{h}"))
+            nc.tensor.matmul(angle_b[h][:], w_b[:], looked_up, start=True, stop=True)
 
-        trig = {name: held.tile([K, N], F32, name=name) for name in ("cos_a", "cos_b", "sin_a", "sin_b")}
-        sources = {
-            "cos_a": (angle_a, cos_bias[:, 0:1]),
-            "sin_a": (angle_a, sin_bias[:, 0:1]),
-            "cos_b": (angle_b, cos_bias[:, 1:2]),
-            "sin_b": (angle_b, sin_bias[:, 1:2]),
-        }
-
-        def half_angle_sine(name):
-            angle, bias = sources[name]
-            nc.scalar.activation(trig[name][:], angle[:], SIN, bias=bias, scale=0.5)
+        cos_a = held.tile([K, N], F32, name="cos_a")
+        sin_a = held.tile([K, N], F32, name="sin_a")
+        cos_b = held.tile([K, N], F32, name="cos_b")
+        sin_b = held.tile([K, N], F32, name="sin_b")
+        for h, piece in enumerate(pieces):
+            nc.scalar.activation(cos_a[:, piece], angle_a[h][:], SIN, bias=cos_bias[:, 0:1], scale=0.5)
+            nc.scalar.activation(cos_b[:, piece], angle_b[h][:], SIN, bias=cos_bias[:, 1:2], scale=0.5)
+        for h, piece in enumerate(pieces):
+            nc.scalar.activation(sin_a[:, piece], angle_a[h][:], SIN, bias=sin_bias[:, 0:1], scale=0.5)
+        for h, piece in enumerate(pieces):
+            nc.scalar.activation(sin_b[:, piece], angle_b[h][:], SIN, bias=sin_bias[:, 1:2], scale=0.5)
+        factors = ((cos_a, cos_b), (cos_a, sin_b), (sin_a, cos_b), (sin_a, sin_b))
 
         planes = out.rearrange("(e k) j -> e k j", k=K)
 
-        factors = (("cos_a", "cos_b"), ("cos_a", "sin_b"), ("sin_a", "cos_b"), ("sin_a", "sin_b"))
-        new_sines = (("cos_a", "cos_b"), ("sin_b",), ("sin_a",), ())
-        for name in new_sines[0]:
-            half_angle_sine(name)
-        v = []
-        for q in range(4):
-            for name in new_sines[q + 1] if q < 3 else ():
-                half_angle_sine(name)
+        v = {}
+        for q in (0, 2, 1, 3):
             of_a, of_b = factors[q]
             term = held.tile([K, N], F32, name=f"v{q}")
-            if q < 3:
-                nc.vector.tensor_tensor(term[:], trig[of_a][:], trig[of_b][:], MULT)
-            else:
-                nc.vector.scalar_tensor_tensor(term[:], trig[of_a][:], -1.0, trig[of_b][:], MULT, MULT)
-            v.append(term)
             square = held.tile([K, N], F32, name=f"square{q}")
-            nc.scalar.activation(square[:], term[:], SQUARE)
+            for piece in pieces:
+                if q < 3:
+                    nc.vector.tensor_tensor(term[:, piece], of_a[:, piece], of_b[:, piece], MULT)
+                else:
+                    nc.vector.scalar_tensor_tensor(term[:, piece], of_a[:, piece], -1.0, of_b[:, piece], MULT, MULT)
+                nc.scalar.activation(square[:, piece], term[:, piece], SQUARE)
             nc.sync.dma_start(planes[5 * q], square[:])
-            for r in range(q):
+            for r in v:
                 product = held.tile([K, N], F32, name=f"product{r}{q}")
-                nc.vector.tensor_tensor(product[:], v[r][:], term[:], MULT)
+                for piece in pieces:
+                    nc.vector.tensor_tensor(product[:, piece], v[r][:, piece], term[:, piece], MULT)
                 for row, col in ((r, q), (q, r)):
                     if (row, col) in NEGATED:
                         minus = held.tile([K, N], F32, name=f"minus{r}{q}")
-                        nc.scalar.mul(minus[:], product[:], -1.0)
+                        for piece in pieces:
+                            nc.scalar.mul(minus[:, piece], product[:, piece], -1.0)
                         nc.sync.dma_start(planes[4 * row + col], minus[:])
                     else:
                         nc.sync.dma_start(planes[4 * row + col], product[:])
+            v[q] = term

@@ -8,9 +8,9 @@ MULT, ADD = mybir.AluOpType.mult, mybir.AluOpType.add
 
 D, S, M, N = 128, 512, 256, 256
 K = M // 2
-FLOPS = 2 * D * M * N
 NEGATED = ((1, 0), (2, 0), (1, 3), (2, 3))
-H = 128
+PIECE = 128
+FLOPS = 2 * D * M * N
 
 
 def tile_featureencodinglayer_kernel(tc, table, w, b, offs, out):
@@ -33,23 +33,23 @@ def tile_featureencodinglayer_kernel(tc, table, w, b, offs, out):
         nc.vector.memset(scratch[:], 0.0)
         nc.scalar.activation(scratch[:], scratch[:], SIN)
 
-        sin_bias = held.tile([K, 2], F32, name="sin_bias")
-        nc.vector.tensor_scalar(sin_bias[:], b_sb[:], 0.5, None, MULT)
         cos_bias = held.tile([K, 2], F32, name="cos_bias")
         nc.vector.tensor_scalar(cos_bias[:], b_sb[:], 0.5, math.pi / 2, MULT, ADD)
+        sin_bias = held.tile([K, 2], F32, name="sin_bias")
+        nc.vector.tensor_scalar(sin_bias[:], b_sb[:], 0.5, None, MULT)
 
-        pieces = [slice(h * H, (h + 1) * H) for h in range(N // H)]
+        pieces = [slice(h * PIECE, (h + 1) * PIECE) for h in range(N // PIECE)]
         angle_a, angle_b = [], []
-        for h in range(N // H):
-            looked_up = table_sb[:].indirect(offsets[:, h * (H // 16) : (h + 1) * (H // 16)])
-            angle_a.append(psum.tile([K, H], F32, name=f"angle_a{h}"))
+        for h in range(N // PIECE):
+            looked_up = table_sb[:].indirect(offsets[:, h * (PIECE // 16) : (h + 1) * (PIECE // 16)])
+            angle_a.append(psum.tile([K, PIECE], F32, name=f"angle_a{h}"))
             nc.tensor.matmul(angle_a[h][:], w_a[:], looked_up, start=True, stop=True)
-            angle_b.append(psum.tile([K, H], F32, name=f"angle_b{h}"))
+            angle_b.append(psum.tile([K, PIECE], F32, name=f"angle_b{h}"))
             nc.tensor.matmul(angle_b[h][:], w_b[:], looked_up, start=True, stop=True)
 
         cos_a = held.tile([K, N], F32, name="cos_a")
-        sin_a = held.tile([K, N], F32, name="sin_a")
         cos_b = held.tile([K, N], F32, name="cos_b")
+        sin_a = held.tile([K, N], F32, name="sin_a")
         sin_b = held.tile([K, N], F32, name="sin_b")
         for h, piece in enumerate(pieces):
             nc.scalar.activation(cos_a[:, piece], angle_a[h][:], SIN, bias=cos_bias[:, 0:1], scale=0.5)
@@ -60,7 +60,7 @@ def tile_featureencodinglayer_kernel(tc, table, w, b, offs, out):
             nc.scalar.activation(sin_b[:, piece], angle_b[h][:], SIN, bias=sin_bias[:, 1:2], scale=0.5)
         factors = ((cos_a, cos_b), (cos_a, sin_b), (sin_a, cos_b), (sin_a, sin_b))
 
-        planes = out.rearrange("(e k) j -> e k j", k=K)
+        planes = out.rearrange("(e k) j -> k e j", k=K)
 
         v = {}
         for q in (0, 2, 1, 3):
@@ -73,17 +73,14 @@ def tile_featureencodinglayer_kernel(tc, table, w, b, offs, out):
                 else:
                     nc.vector.scalar_tensor_tensor(term[:, piece], of_a[:, piece], -1.0, of_b[:, piece], MULT, MULT)
                 nc.scalar.activation(square[:, piece], term[:, piece], SQUARE)
-            nc.sync.dma_start(planes[5 * q], square[:])
+            nc.sync.dma_start(planes[:, 4 * q + q, :], square[:])
             for r in v:
-                product = held.tile([K, N], F32, name=f"product{r}{q}")
+                lo, hi = min(r, q), max(r, q)
+                mirrors = held.tile([K, 2, N], F32, name=f"mirrors{lo}{hi}")
+                plain = 1 if (lo, hi) in NEGATED else 0
+                sign = -1.0 if (lo, hi) in NEGATED or (hi, lo) in NEGATED else 1.0
                 for piece in pieces:
-                    nc.vector.tensor_tensor(product[:, piece], v[r][:, piece], term[:, piece], MULT)
-                for row, col in ((r, q), (q, r)):
-                    if (row, col) in NEGATED:
-                        minus = held.tile([K, N], F32, name=f"minus{r}{q}")
-                        for piece in pieces:
-                            nc.scalar.mul(minus[:, piece], product[:, piece], -1.0)
-                        nc.sync.dma_start(planes[4 * row + col], minus[:])
-                    else:
-                        nc.sync.dma_start(planes[4 * row + col], product[:])
+                    nc.vector.tensor_tensor(mirrors[:, plain, piece], v[r][:, piece], term[:, piece], MULT)
+                    nc.scalar.mul(mirrors[:, 1 - plain, piece], mirrors[:, plain, piece], sign)
+                nc.sync.dma_start(planes[:, 4 * lo + hi : 4 * hi + lo + 1 : 3 * (hi - lo), :], mirrors[:])
             v[q] = term

@@ -8,7 +8,6 @@ MULT, ADD = mybir.AluOpType.mult, mybir.AluOpType.add
 
 D, S, M, N = 128, 512, 256, 256
 K = M // 2
-NEGATED = ((1, 0), (2, 0), (1, 3), (2, 3))
 PIECE = 128
 FLOPS = 2 * D * M * N
 
@@ -35,8 +34,6 @@ def tile_featureencodinglayer_kernel(tc, table, w, b, offs, out):
 
         cos_bias = held.tile([K, 2], F32, name="cos_bias")
         nc.vector.tensor_scalar(cos_bias[:], b_sb[:], 0.5, math.pi / 2, MULT, ADD)
-        sin_bias = held.tile([K, 2], F32, name="sin_bias")
-        nc.vector.tensor_scalar(sin_bias[:], b_sb[:], 0.5, None, MULT)
 
         pieces = [slice(h * PIECE, (h + 1) * PIECE) for h in range(N // PIECE)]
         angle_a, angle_b = [], []
@@ -47,40 +44,63 @@ def tile_featureencodinglayer_kernel(tc, table, w, b, offs, out):
             angle_b.append(psum.tile([K, PIECE], F32, name=f"angle_b{h}"))
             nc.tensor.matmul(angle_b[h][:], w_b[:], looked_up, start=True, stop=True)
 
-        cos_a = held.tile([K, N], F32, name="cos_a")
-        cos_b = held.tile([K, N], F32, name="cos_b")
+        e_sb = held.tile([K, 16, N], F32, name="e_sb")
+        planes = out.rearrange("(e k) j -> k e j", k=K)
+
+        def product(e, in0, factor, in1):
+            for piece in pieces:
+                nc.vector.scalar_tensor_tensor(e_sb[:, e, piece], in0[:, piece], factor, in1[:, piece], MULT, MULT)
+
+        def negated(e, of):
+            for piece in pieces:
+                nc.scalar.mul(e_sb[:, e, piece], e_sb[:, of, piece], -1.0)
+
+        def store(first, last, step):
+            nc.sync.dma_start(planes[:, first : last + 1 : step, :], e_sb[:, first : last + 1 : step, :])
+
         sin_a = held.tile([K, N], F32, name="sin_a")
         sin_b = held.tile([K, N], F32, name="sin_b")
         for h, piece in enumerate(pieces):
+            nc.scalar.activation(sin_a[:, piece], angle_a[h][:], SIN, bias=b_sb[:, 0:1], scale=1.0)
+            nc.scalar.activation(sin_b[:, piece], angle_b[h][:], SIN, bias=b_sb[:, 1:2], scale=1.0)
+            nc.vector.scalar_tensor_tensor(e_sb[:, 6, piece], sin_a[:, piece], 0.25, sin_b[:, piece], MULT, MULT)
+            nc.vector.tensor_scalar(e_sb[:, 3, piece], e_sb[:, 6, piece], -1.0, None, MULT)
+        nc.sync.dma_start(planes[:, 6:10:3, :], e_sb[:, 6:7, :].to_broadcast([K, 2, N]))
+        nc.sync.dma_start(planes[:, 3:13:9, :], e_sb[:, 3:4, :].to_broadcast([K, 2, N]))
+
+        cos_a = held.tile([K, N], F32, name="cos_a")
+        c_a = held.tile([K, N], F32, name="c_a")
+        for h, piece in enumerate(pieces):
             nc.scalar.activation(cos_a[:, piece], angle_a[h][:], SIN, bias=cos_bias[:, 0:1], scale=0.5)
+            nc.scalar.activation(c_a[:, piece], cos_a[:, piece], SQUARE)
+        product(1, c_a, 0.5, sin_b)
+        negated(4, of=1)
+        store(1, 4, 3)
+
+        cos_b = held.tile([K, N], F32, name="cos_b")
+        c_b = held.tile([K, N], F32, name="c_b")
+        for h, piece in enumerate(pieces):
             nc.scalar.activation(cos_b[:, piece], angle_b[h][:], SIN, bias=cos_bias[:, 1:2], scale=0.5)
-        for h, piece in enumerate(pieces):
-            nc.scalar.activation(sin_a[:, piece], angle_a[h][:], SIN, bias=sin_bias[:, 0:1], scale=0.5)
-        for h, piece in enumerate(pieces):
-            nc.scalar.activation(sin_b[:, piece], angle_b[h][:], SIN, bias=sin_bias[:, 1:2], scale=0.5)
-        factors = ((cos_a, cos_b), (cos_a, sin_b), (sin_a, cos_b), (sin_a, sin_b))
+            nc.scalar.activation(c_b[:, piece], cos_b[:, piece], SQUARE)
+        product(2, sin_a, 0.5, c_b)
+        negated(8, of=2)
+        store(2, 8, 6)
+        product(0, c_a, 1.0, c_b)
+        store(0, 0, 1)
 
-        planes = out.rearrange("(e k) j -> k e j", k=K)
+        s_a = held.tile([K, N], F32, name="s_a")
+        nc.vector.tensor_scalar(s_a[:], c_a[:], -1.0, 1.0, MULT, ADD)
+        product(11, s_a, 0.5, sin_b)
+        negated(14, of=11)
+        store(11, 14, 3)
 
-        v = {}
-        for q in (0, 2, 1, 3):
-            of_a, of_b = factors[q]
-            term = held.tile([K, N], F32, name=f"v{q}")
-            square = held.tile([K, N], F32, name=f"square{q}")
-            for piece in pieces:
-                if q < 3:
-                    nc.vector.tensor_tensor(term[:, piece], of_a[:, piece], of_b[:, piece], MULT)
-                else:
-                    nc.vector.scalar_tensor_tensor(term[:, piece], of_a[:, piece], -1.0, of_b[:, piece], MULT, MULT)
-                nc.scalar.activation(square[:, piece], term[:, piece], SQUARE)
-            nc.sync.dma_start(planes[:, 4 * q + q, :], square[:])
-            for r in v:
-                lo, hi = min(r, q), max(r, q)
-                mirrors = held.tile([K, 2, N], F32, name=f"mirrors{lo}{hi}")
-                plain = 1 if (lo, hi) in NEGATED else 0
-                sign = -1.0 if (lo, hi) in NEGATED or (hi, lo) in NEGATED else 1.0
-                for piece in pieces:
-                    nc.vector.tensor_tensor(mirrors[:, plain, piece], v[r][:, piece], term[:, piece], MULT)
-                    nc.scalar.mul(mirrors[:, 1 - plain, piece], mirrors[:, plain, piece], sign)
-                nc.sync.dma_start(planes[:, 4 * lo + hi : 4 * hi + lo + 1 : 3 * (hi - lo), :], mirrors[:])
-            v[q] = term
+        s_b = held.tile([K, N], F32, name="s_b")
+        nc.vector.tensor_scalar(s_b[:], c_b[:], -1.0, 1.0, MULT, ADD)
+        product(7, sin_a, 0.5, s_b)
+        negated(13, of=7)
+        store(7, 13, 6)
+
+        product(5, c_a, 1.0, s_b)
+        product(10, s_a, 1.0, c_b)
+        product(15, s_a, 1.0, s_b)
+        store(5, 15, 5)

@@ -102,5 +102,6 @@ def tile_featureencodinglayer_kernel(tc, table, w, b, offs, out):
 
         product(5, c_a, 1.0, s_b)
         product(10, s_a, 1.0, c_b)
+        store(5, 10, 5)
         product(15, s_a, 1.0, s_b)
-        store(5, 15, 5)
+        store(15, 15, 1)

@@ -69,19 +69,20 @@ def tile_featureencodinglayer_kernel(tc, table, w, b, offs, out):
         nc.sync.dma_start(planes[:, 3:13:9, :], e_sb[:, 3:4, :].to_broadcast([K, 2, N]))
 
         cos_a = held.tile([K, N], F32, name="cos_a")
+        cos_b = held.tile([K, N], F32, name="cos_b")
         c_a = held.tile([K, N], F32, name="c_a")
+        c_b = held.tile([K, N], F32, name="c_b")
         for h, piece in enumerate(pieces):
             nc.scalar.activation(cos_a[:, piece], angle_a[h][:], SIN, bias=cos_bias[:, 0:1], scale=0.5)
-            nc.scalar.activation(c_a[:, piece], cos_a[:, piece], SQUARE)
+            nc.vector.tensor_tensor(c_a[:, piece], cos_a[:, piece], cos_a[:, piece], MULT)
+        for h, piece in enumerate(pieces):
+            nc.scalar.activation(cos_b[:, piece], angle_b[h][:], SIN, bias=cos_bias[:, 1:2], scale=0.5)
+        for piece in pieces:
+            nc.scalar.activation(c_b[:, piece], cos_b[:, piece], SQUARE)
+
         product(1, c_a, 0.5, sin_b)
         negated(4, of=1)
         store(1, 4, 3)
-
-        cos_b = held.tile([K, N], F32, name="cos_b")
-        c_b = held.tile([K, N], F32, name="c_b")
-        for h, piece in enumerate(pieces):
-            nc.scalar.activation(cos_b[:, piece], angle_b[h][:], SIN, bias=cos_bias[:, 1:2], scale=0.5)
-            nc.scalar.activation(c_b[:, piece], cos_b[:, piece], SQUARE)
         product(2, sin_a, 0.5, c_b)
         negated(8, of=2)
         store(2, 8, 6)
@@ -90,16 +91,14 @@ def tile_featureencodinglayer_kernel(tc, table, w, b, offs, out):
 
         s_a = held.tile([K, N], F32, name="s_a")
         nc.vector.tensor_scalar(s_a[:], c_a[:], -1.0, 1.0, MULT, ADD)
+        s_b = held.tile([K, N], F32, name="s_b")
+        nc.vector.tensor_scalar(s_b[:], c_b[:], -1.0, 1.0, MULT, ADD)
         product(11, s_a, 0.5, sin_b)
         negated(14, of=11)
         store(11, 14, 3)
-
-        s_b = held.tile([K, N], F32, name="s_b")
-        nc.vector.tensor_scalar(s_b[:], c_b[:], -1.0, 1.0, MULT, ADD)
         product(7, sin_a, 0.5, s_b)
         negated(13, of=7)
         store(7, 13, 6)
-
         product(5, c_a, 1.0, s_b)
         product(10, s_a, 1.0, c_b)
         store(5, 10, 5)

@@ -64,8 +64,8 @@ def tile_featureencodinglayer_kernel(tc, table, w, b, offs, out):
             nc.scalar.activation(sin_a[:, piece], angle_a[h][:], SIN, bias=b_sb[:, 0:1], scale=1.0)
             nc.scalar.activation(sin_b[:, piece], angle_b[h][:], SIN, bias=b_sb[:, 1:2], scale=1.0)
             nc.vector.scalar_tensor_tensor(e_sb[:, 6, piece], sin_a[:, piece], 0.25, sin_b[:, piece], MULT, MULT)
+            nc.sync.dma_start(planes[:, 6:10:3, piece], e_sb[:, 6:7, piece].to_broadcast([K, 2, PIECE]))
             nc.vector.tensor_scalar(e_sb[:, 3, piece], e_sb[:, 6, piece], -1.0, None, MULT)
-        nc.sync.dma_start(planes[:, 6:10:3, :], e_sb[:, 6:7, :].to_broadcast([K, 2, N]))
         nc.sync.dma_start(planes[:, 3:13:9, :], e_sb[:, 3:4, :].to_broadcast([K, 2, N]))
 
         cos_a = held.tile([K, N], F32, name="cos_a")

@@ -21,10 +21,6 @@ def tile_featureencodinglayer_kernel(tc, table, w, b, offs, out):
         nc.sync.dma_start(table_sb[:], table)
         w_sb = held.tile([D, K, 2], BF16, name="w_sb")
         nc.scalar.dma_start(w_sb[:], w.rearrange("d (k u) -> d k u", u=2))
-        w_a = held.tile([D, K], BF16, name="w_a")
-        nc.vector.tensor_copy(w_a[:], w_sb[:, :, 0])
-        w_b = held.tile([D, K], BF16, name="w_b")
-        nc.vector.tensor_copy(w_b[:], w_sb[:, :, 1])
         b_sb = held.tile([K, 2], F32, name="b_sb")
         nc.scalar.dma_start(b_sb[:], b.rearrange("(k u) o -> k (u o)", u=2))
 
@@ -40,9 +36,9 @@ def tile_featureencodinglayer_kernel(tc, table, w, b, offs, out):
         for h in range(N // PIECE):
             looked_up = table_sb[:].indirect(offsets[:, h * (PIECE // 16) : (h + 1) * (PIECE // 16)])
             angle_a.append(psum.tile([K, PIECE], F32, name=f"angle_a{h}"))
-            nc.tensor.matmul(angle_a[h][:], w_a[:], looked_up, start=True, stop=True)
+            nc.tensor.matmul(angle_a[h][:], w_sb[:, :, 0], looked_up, start=True, stop=True)
             angle_b.append(psum.tile([K, PIECE], F32, name=f"angle_b{h}"))
-            nc.tensor.matmul(angle_b[h][:], w_b[:], looked_up, start=True, stop=True)
+            nc.tensor.matmul(angle_b[h][:], w_sb[:, :, 1], looked_up, start=True, stop=True)
 
         e_sb = held.tile([K, 16, N], F32, name="e_sb")
         planes = out.rearrange("(e k) j -> k e j", k=K)

@@ -15,10 +15,10 @@ FLOPS = 2 * D * M * N
 def tile_featureencodinglayer_kernel(tc, table, w, b, offs, out):
     nc = tc.nc
     with tc.tile_pool(name="held", bufs=1) as held, tc.psum_pool(name="psum", bufs=1) as psum:
-        offsets = held.tile([128, N // 16], U16, name="offsets")
-        nc.sync.dma_start(offsets[:], offs)
         table_sb = held.tile([D, S], BF16, name="table_sb")
         nc.sync.dma_start(table_sb[:], table)
+        offsets = held.tile([128, N // 16], U16, name="offsets")
+        nc.sync.dma_start(offsets[:], offs)
         w_sb = held.tile([D, K, 2], BF16, name="w_sb")
         nc.scalar.dma_start(w_sb[:], w.rearrange("d (k u) -> d k u", u=2))
         b_sb = held.tile([K, 2], F32, name="b_sb")

@@ -4,6 +4,7 @@ import concourse.mybir as mybir
 
 F32, BF16, U16 = mybir.dt.float32, mybir.dt.bfloat16, mybir.dt.uint16
 SIN, SQUARE = mybir.ActivationFunctionType.Sin, mybir.ActivationFunctionType.Square
+COPY = mybir.ActivationFunctionType.Copy
 MULT, ADD = mybir.AluOpType.mult, mybir.AluOpType.add
 
 D, S, M, N = 128, 512, 256, 256
@@ -48,8 +49,7 @@ def tile_featureencodinglayer_kernel(tc, table, w, b, offs, out):
                 nc.vector.scalar_tensor_tensor(e_sb[:, e, piece], in0[:, piece], factor, in1[:, piece], MULT, MULT)
 
         def negated(e, of):
-            for piece in pieces:
-                nc.scalar.mul(e_sb[:, e, piece], e_sb[:, of, piece], -1.0)
+            nc.vector.tensor_scalar(e_sb[:, e, :], e_sb[:, of, :], -1.0, None, MULT)
 
         def store(first, last, step):
             nc.sync.dma_start(planes[:, first : last + 1 : step, :], e_sb[:, first : last + 1 : step, :])
@@ -76,6 +76,11 @@ def tile_featureencodinglayer_kernel(tc, table, w, b, offs, out):
         for piece in pieces:
             nc.scalar.activation(c_b[:, piece], cos_b[:, piece], SQUARE)
 
+        s_a = held.tile([K, N], F32, name="s_a")
+        s_b = held.tile([K, N], F32, name="s_b")
+        nc.scalar.activation(s_a[:], c_a[:], COPY, bias=1.0, scale=-1.0)
+        nc.scalar.activation(s_b[:], c_b[:], COPY, bias=1.0, scale=-1.0)
+
         product(1, c_a, 0.5, sin_b)
         negated(4, of=1)
         store(1, 4, 3)
@@ -85,10 +90,6 @@ def tile_featureencodinglayer_kernel(tc, table, w, b, offs, out):
         product(0, c_a, 1.0, c_b)
         store(0, 0, 1)
 
-        s_a = held.tile([K, N], F32, name="s_a")
-        nc.vector.tensor_scalar(s_a[:], c_a[:], -1.0, 1.0, MULT, ADD)
-        s_b = held.tile([K, N], F32, name="s_b")
-        nc.vector.tensor_scalar(s_b[:], c_b[:], -1.0, 1.0, MULT, ADD)
         product(11, s_a, 0.5, sin_b)
         negated(14, of=11)
         store(11, 14, 3)

@@ -44,60 +44,64 @@ def tile_featureencodinglayer_kernel(tc, table, w, b, offs, out):
         e_sb = held.tile([K, 16, N], F32, name="e_sb")
         planes = out.rearrange("(e k) j -> k e j", k=K)
 
+        def product_of_piece(e, in0, factor, in1, piece):
+            nc.vector.scalar_tensor_tensor(e_sb[:, e, piece], in0[:, piece], factor, in1[:, piece], MULT, MULT)
+
         def product(e, in0, factor, in1):
             for piece in pieces:
-                nc.vector.scalar_tensor_tensor(e_sb[:, e, piece], in0[:, piece], factor, in1[:, piece], MULT, MULT)
+                product_of_piece(e, in0, factor, in1, piece)
 
         def negated(e, of):
-            nc.vector.tensor_scalar(e_sb[:, e, :], e_sb[:, of, :], -1.0, None, MULT)
+            for piece in pieces:
+                nc.scalar.mul(e_sb[:, e, piece], e_sb[:, of, piece], -1.0)
 
         def store(first, last, step):
             nc.sync.dma_start(planes[:, first : last + 1 : step, :], e_sb[:, first : last + 1 : step, :])
 
         sin_a = held.tile([K, N], F32, name="sin_a")
         sin_b = held.tile([K, N], F32, name="sin_b")
-        for h, piece in enumerate(pieces):
-            nc.scalar.activation(sin_a[:, piece], angle_a[h][:], SIN, bias=b_sb[:, 0:1], scale=1.0)
-            nc.scalar.activation(sin_b[:, piece], angle_b[h][:], SIN, bias=b_sb[:, 1:2], scale=1.0)
-            nc.vector.scalar_tensor_tensor(e_sb[:, 6, piece], sin_a[:, piece], 0.25, sin_b[:, piece], MULT, MULT)
-            nc.sync.dma_start(planes[:, 6:10:3, piece], e_sb[:, 6:7, piece].to_broadcast([K, 2, PIECE]))
-            nc.vector.tensor_scalar(e_sb[:, 3, piece], e_sb[:, 6, piece], -1.0, None, MULT)
-        nc.sync.dma_start(planes[:, 3:13:9, :], e_sb[:, 3:4, :].to_broadcast([K, 2, N]))
-
         cos_a = held.tile([K, N], F32, name="cos_a")
         cos_b = held.tile([K, N], F32, name="cos_b")
         c_a = held.tile([K, N], F32, name="c_a")
         c_b = held.tile([K, N], F32, name="c_b")
+        s_a = held.tile([K, N], F32, name="s_a")
+        s_b = held.tile([K, N], F32, name="s_b")
+
         for h, piece in enumerate(pieces):
+            nc.scalar.activation(sin_a[:, piece], angle_a[h][:], SIN, bias=b_sb[:, 0:1], scale=1.0)
+            nc.scalar.activation(sin_b[:, piece], angle_b[h][:], SIN, bias=b_sb[:, 1:2], scale=1.0)
             nc.scalar.activation(cos_a[:, piece], angle_a[h][:], SIN, bias=cos_bias[:, 0:1], scale=0.5)
+            product_of_piece(6, sin_a, 0.25, sin_b, piece)
+            nc.sync.dma_start(planes[:, 6:10:3, piece], e_sb[:, 6:7, piece].to_broadcast([K, 2, PIECE]))
+            product_of_piece(3, sin_a, -0.25, sin_b, piece)
             nc.vector.tensor_tensor(c_a[:, piece], cos_a[:, piece], cos_a[:, piece], MULT)
+        nc.sync.dma_start(planes[:, 3:13:9, :], e_sb[:, 3:4, :].to_broadcast([K, 2, N]))
+
+        for piece in pieces:
+            product_of_piece(1, c_a, 0.5, sin_b, piece)
+            product_of_piece(4, c_a, -0.5, sin_b, piece)
+        store(1, 4, 3)
+
         for h, piece in enumerate(pieces):
             nc.scalar.activation(cos_b[:, piece], angle_b[h][:], SIN, bias=cos_bias[:, 1:2], scale=0.5)
         for piece in pieces:
             nc.scalar.activation(c_b[:, piece], cos_b[:, piece], SQUARE)
-
-        s_a = held.tile([K, N], F32, name="s_a")
-        s_b = held.tile([K, N], F32, name="s_b")
         nc.scalar.activation(s_a[:], c_a[:], COPY, bias=1.0, scale=-1.0)
         nc.scalar.activation(s_b[:], c_b[:], COPY, bias=1.0, scale=-1.0)
 
-        product(1, c_a, 0.5, sin_b)
-        negated(4, of=1)
-        store(1, 4, 3)
         product(2, sin_a, 0.5, c_b)
         negated(8, of=2)
-        store(2, 8, 6)
+        store(2, 2, 1)
         product(0, c_a, 1.0, c_b)
-        store(0, 0, 1)
-
+        store(0, 8, 8)
         product(11, s_a, 0.5, sin_b)
         negated(14, of=11)
-        store(11, 14, 3)
+        store(11, 11, 1)
         product(7, sin_a, 0.5, s_b)
         negated(13, of=7)
-        store(7, 13, 6)
-        product(5, c_a, 1.0, s_b)
+        store(7, 14, 7)
         product(10, s_a, 1.0, c_b)
-        store(5, 10, 5)
+        store(10, 13, 3)
+        product(5, c_a, 1.0, s_b)
         product(15, s_a, 1.0, s_b)
-        store(15, 15, 1)
+        store(5, 15, 10)

@@ -70,17 +70,18 @@ def tile_featureencodinglayer_kernel(tc, table, w, b, offs, out):
         for h, piece in enumerate(pieces):
             nc.scalar.activation(sin_a[:, piece], angle_a[h][:], SIN, bias=b_sb[:, 0:1], scale=1.0)
             nc.scalar.activation(sin_b[:, piece], angle_b[h][:], SIN, bias=b_sb[:, 1:2], scale=1.0)
-            nc.scalar.activation(cos_a[:, piece], angle_a[h][:], SIN, bias=cos_bias[:, 0:1], scale=0.5)
             product_of_piece(6, sin_a, 0.25, sin_b, piece)
             nc.sync.dma_start(planes[:, 6:10:3, piece], e_sb[:, 6:7, piece].to_broadcast([K, 2, PIECE]))
             product_of_piece(3, sin_a, -0.25, sin_b, piece)
-            nc.vector.tensor_tensor(c_a[:, piece], cos_a[:, piece], cos_a[:, piece], MULT)
         nc.sync.dma_start(planes[:, 3:13:9, :], e_sb[:, 3:4, :].to_broadcast([K, 2, N]))
 
-        for piece in pieces:
-            product_of_piece(1, c_a, 0.5, sin_b, piece)
-            product_of_piece(4, c_a, -0.5, sin_b, piece)
-        store(1, 4, 3)
+        for h, piece in enumerate(pieces):
+            nc.scalar.activation(cos_a[:, piece], angle_a[h][:], SIN, bias=cos_bias[:, 0:1], scale=0.5)
+            nc.vector.tensor_tensor(c_a[:, piece], cos_a[:, piece], cos_a[:, piece], MULT)
+        product(1, c_a, 0.5, sin_b)
+        store(1, 1, 1)
+        product(4, c_a, -0.5, sin_b)
+        store(4, 4, 1)
 
         for h, piece in enumerate(pieces):
             nc.scalar.activation(cos_b[:, piece], angle_b[h][:], SIN, bias=cos_bias[:, 1:2], scale=0.5)

import math

import concourse.mybir as mybir

F32, BF16, U16 = mybir.dt.float32, mybir.dt.bfloat16, mybir.dt.uint16
SIN, SQUARE = mybir.ActivationFunctionType.Sin, mybir.ActivationFunctionType.Square
COPY = mybir.ActivationFunctionType.Copy
MULT, ADD = mybir.AluOpType.mult, mybir.AluOpType.add

D, S, M, N = 128, 512, 256, 256
K = M // 2
PIECE = 128
FLOPS = 2 * D * M * N


def tile_featureencodinglayer_kernel(tc, table, w, b, offs, out):
    nc = tc.nc
    with tc.tile_pool(name="held", bufs=1) as held, tc.psum_pool(name="psum", bufs=1) as psum:
        table_sb = held.tile([D, S], BF16, name="table_sb")
        nc.sync.dma_start(table_sb[:], table)
        offsets = held.tile([128, N // 16], U16, name="offsets")
        nc.sync.dma_start(offsets[:], offs)
        w_sb = held.tile([D, K, 2], BF16, name="w_sb")
        nc.scalar.dma_start(w_sb[:], w.rearrange("d (k u) -> d k u", u=2))
        b_sb = held.tile([K, 2], F32, name="b_sb")
        nc.scalar.dma_start(b_sb[:], b.rearrange("(k u) o -> k (u o)", u=2))

        scratch = held.tile([K, 1], F32, name="scratch")
        nc.vector.memset(scratch[:], 0.0)
        nc.scalar.activation(scratch[:], scratch[:], SIN)

        cos_bias = held.tile([K, 2], F32, name="cos_bias")
        nc.vector.tensor_scalar(cos_bias[:], b_sb[:], 0.5, math.pi / 2, MULT, ADD)

        pieces = [slice(h * PIECE, (h + 1) * PIECE) for h in range(N // PIECE)]
        angle_a, angle_b = [], []
        for h in range(N // PIECE):
            looked_up = table_sb[:].indirect(offsets[:, h * (PIECE // 16) : (h + 1) * (PIECE // 16)])
            angle_a.append(psum.tile([K, PIECE], F32, name=f"angle_a{h}"))
            nc.tensor.matmul(angle_a[h][:], w_sb[:, :, 0], looked_up, start=True, stop=True)
            angle_b.append(psum.tile([K, PIECE], F32, name=f"angle_b{h}"))
            nc.tensor.matmul(angle_b[h][:], w_sb[:, :, 1], looked_up, start=True, stop=True)

        e_sb = held.tile([K, 16, N], F32, name="e_sb")
        planes = out.rearrange("(e k) j -> k e j", k=K)

        def product_of_piece(e, in0, factor, in1, piece):
            nc.vector.scalar_tensor_tensor(e_sb[:, e, piece], in0[:, piece], factor, in1[:, piece], MULT, MULT)

        def product(e, in0, factor, in1):
            for piece in pieces:
                product_of_piece(e, in0, factor, in1, piece)

        def negated(e, of):
            for piece in pieces:
                nc.scalar.mul(e_sb[:, e, piece], e_sb[:, of, piece], -1.0)

        def store(first, last, step):
            nc.sync.dma_start(planes[:, first : last + 1 : step, :], e_sb[:, first : last + 1 : step, :])

        sin_a = held.tile([K, N], F32, name="sin_a")
        sin_b = held.tile([K, N], F32, name="sin_b")
        cos_a = held.tile([K, N], F32, name="cos_a")
        cos_b = held.tile([K, N], F32, name="cos_b")
        c_a = held.tile([K, N], F32, name="c_a")
        c_b = held.tile([K, N], F32, name="c_b")
        s_a = held.tile([K, N], F32, name="s_a")
        s_b = held.tile([K, N], F32, name="s_b")

        for h, piece in enumerate(pieces):
            nc.scalar.activation(sin_a[:, piece], angle_a[h][:], SIN, bias=b_sb[:, 0:1], scale=1.0)
            nc.scalar.activation(sin_b[:, piece], angle_b[h][:], SIN, bias=b_sb[:, 1:2], scale=1.0)
            product_of_piece(6, sin_a, 0.25, sin_b, piece)
            nc.sync.dma_start(planes[:, 6:10:3, piece], e_sb[:, 6:7, piece].to_broadcast([K, 2, PIECE]))
            product_of_piece(3, sin_a, -0.25, sin_b, piece)
        nc.sync.dma_start(planes[:, 3:13:9, :], e_sb[:, 3:4, :].to_broadcast([K, 2, N]))

        for h, piece in enumerate(pieces):
            nc.scalar.activation(cos_a[:, piece], angle_a[h][:], SIN, bias=cos_bias[:, 0:1], scale=0.5)
            nc.vector.tensor_tensor(c_a[:, piece], cos_a[:, piece], cos_a[:, piece], MULT)
        product(1, c_a, 0.5, sin_b)
        store(1, 1, 1)
        product(4, c_a, -0.5, sin_b)
        store(4, 4, 1)

        for h, piece in enumerate(pieces):
            nc.scalar.activation(cos_b[:, piece], angle_b[h][:], SIN, bias=cos_bias[:, 1:2], scale=0.5)
        for piece in pieces:
            nc.scalar.activation(c_b[:, piece], cos_b[:, piece], SQUARE)
        nc.scalar.activation(s_a[:], c_a[:], COPY, bias=1.0, scale=-1.0)
        nc.scalar.activation(s_b[:], c_b[:], COPY, bias=1.0, scale=-1.0)

        product(2, sin_a, 0.5, c_b)
        negated(8, of=2)
        store(2, 2, 1)
        product(0, c_a, 1.0, c_b)
        store(0, 8, 8)
        product(11, s_a, 0.5, sin_b)
        negated(14, of=11)
        store(11, 11, 1)
        product(7, sin_a, 0.5, s_b)
        negated(13, of=7)
        store(7, 14, 7)
        product(10, s_a, 1.0, c_b)
        store(10, 13, 3)
        product(5, c_a, 1.0, s_b)
        product(15, s_a, 1.0, s_b)
        store(5, 15, 10)
